import numpy as np
import ml_dtypes


def mxq(x, axis, fmt="e4m3"):
    dtype, down = {"e4m3": (ml_dtypes.float8_e4m3fn, 7), "e5m2": (ml_dtypes.float8_e5m2, 14)}[fmt]
    v = np.moveaxis(np.asarray(x, np.float32).astype(ml_dtypes.bfloat16).astype(np.float64), axis, -1)
    blocks = v.reshape(v.shape[:-1] + (-1, 32))
    amax = np.abs(blocks).max(-1, keepdims=True)
    byte = np.maximum(np.where(amax > 0, np.frexp(amax)[1] - 1 + 127, 0) - down, 1)
    scale = np.exp2(byte - 127.0)
    codes = (blocks / scale).astype(np.float32).astype(dtype).astype(np.float64)
    return np.moveaxis((codes * scale).reshape(v.shape), -1, axis)


WIDE = False


def mx_kscale(k):
    if not WIDE:
        return np.ones(k)
    levels = np.array([10, -10, 5, -5, 0])
    if k % 512:
        return np.exp2(np.random.permutation(np.resize(levels, k // 32))).repeat(32)
    a = np.empty((k // 512, 16))
    for p in range(k // 512):
        a[p, :8] = np.random.permutation(np.resize(levels, 8))
        for g in range(8):
            far = levels[np.abs(levels - a[p, g]) >= 10]
            a[p, g + 8] = far[np.random.randint(len(far))]
    return np.exp2(a.ravel()).repeat(32)


BF16 = ml_dtypes.bfloat16


def bf(x):
    return np.asarray(x, np.float32).astype(BF16)


def f64(x):
    return np.asarray(x).astype(np.float64)


B, IN, HID, OUT, LAYERS, NG = 1024, 512, 1024, 512, 2, 4
GW = NG * HID


def sigmoid(v):
    return 1.0 / (1.0 + np.exp(-v))


def draw0():
    s = mx_kscale(IN)
    return {
        "regime_vector": bf(np.random.standard_normal((B, IN)) * s),
        "W_ih0": bf(np.random.standard_normal((GW, IN)) / np.sqrt(IN) / s),
        "hh_gates": bf(np.random.standard_normal(GW) * 0.5),
        "b_ih0": bf(np.random.standard_normal(GW) * 0.3),
        "b_hh0": bf(np.random.standard_normal(GW) * 0.3),
        "c_init": bf(np.random.standard_normal(HID)),
    }


def core(regime_vector, W_ih0, hh_gates, b_ih0, b_hh0, c_init):
    gates = (mxq(f64(regime_vector), 1, "e4m3") @ mxq(f64(W_ih0).T, 0, "e4m3")) + f64(hh_gates) + (f64(b_ih0) + f64(b_hh0))
    i, f, g, o = np.split(gates, NG, axis=-1)
    i, f, o = sigmoid(i), sigmoid(f), sigmoid(o)
    g = np.tanh(g)
    c_new = f * f64(c_init) + i * g
    return o * np.tanh(c_new)


def e4m3fn_bytes(y):
    return np.clip(np.asarray(y, np.float64), -448.0, 448.0).astype(np.float32).astype(ml_dtypes.float8_e4m3fn).view(np.uint8)


def e4m3fn_values(b):
    return np.asarray(b, np.uint8).view(ml_dtypes.float8_e4m3fn).astype(np.float64)


def setup_inputs():
    d = draw0()
    x0 = np.asarray(d['W_ih0']).astype(np.float64)
    s = (np.max(np.abs(x0), axis=(0,), keepdims=True) / 448.0).astype(np.float32)
    out = {}
    for k, v in d.items():
        if k == 'W_ih0':
            out['W_ih0_bytes'] = e4m3fn_bytes(x0 / s.astype(np.float64))
            out['W_ih0_scale'] = s
        else:
            out[k] = v
    return out


def reference(regime_vector, W_ih0_bytes, W_ih0_scale, hh_gates, b_ih0, b_hh0, c_init):
    return core(regime_vector, e4m3fn_values(W_ih0_bytes) * W_ih0_scale.astype(np.float64), hh_gates, b_ih0, b_hh0, c_init)

@@ -1,0 +1,393 @@
+from contextlib import ExitStack
+
+import concourse.mybir as mybir
+from concourse.masks import make_identity
+
+B, K, HID, NG = 1024, 512, 1024, 4
+FLOPS = 2 * B * K * NG * HID
+
+F32 = mybir.dt.float32
+BF16 = mybir.dt.bfloat16
+U32 = mybir.dt.uint32
+U8 = mybir.dt.uint8
+FP8 = mybir.dt.float8_e4m3fn
+FP8X4 = mybir.dt.float8_e4m3fn_x4
+ACT = mybir.ActivationFunctionType
+ALU = mybir.AluOpType
+
+P = 128
+NH = HID // P
+HALF = 512
+GATE_I, GATE_F, GATE_G, GATE_O = 0, 1, 2, 3
+
+NPAIR = 2 * NH
+GATE_BANKS = 5
+VECTOR_COPIES = (4, 6, 8, 10, 12, 14, 15)
+
+
+def tile_rdecommunicationlstm_pa_kernel(
+    tc, regime_vector, W_ih0_bytes, W_ih0_scale, hh_gates, b_ih0, b_hh0, c_init, out
+):
+    nc = tc.nc
+
+    x_view = regime_vector.rearrange("(b j p) k -> b p j k", b=4, j=2, p=P)
+    w_view = W_ih0_bytes.rearrange("(a q h p) k -> q h p a k", a=2, q=2, h=NH, p=P)
+    out_view = out.rearrange("(t j p) c -> t p j c", t=2, j=4, p=P)
+
+    with ExitStack() as ctx:
+        const = ctx.enter_context(tc.tile_pool(name="const", bufs=1))
+        keep = ctx.enter_context(tc.tile_pool(name="keep", bufs=1))
+        prep = ctx.enter_context(tc.tile_pool(name="prep", bufs=3))
+        ep = ctx.enter_context(tc.tile_pool(name="ep", bufs=4))
+        psum = ctx.enter_context(tc.psum_pool(name="psum", bufs=1))
+        ctx.enter_context(tc.manual_schedule())
+
+        warm_in = const.tile([P, 1], F32, name="warm_in")
+        warm_out = const.tile([P, 1], F32, name="warm_out")
+        vec_rows = const.tile([P, P], BF16, name="vec_rows")
+        vec_cols = const.tile([P, P], F32, name="vec_cols")
+        bias_tmp = const.tile([P, NG * NH], F32, name="bias_tmp")
+        bias = const.tile([P, NG * NH], F32, name="bias")
+        ident_f = const.tile([P, P], F32, name="ident_f")
+        ident_b = const.tile([P, P], BF16, name="ident_b")
+        scale2 = const.tile([P, 2, K], F32, name="scale2")
+
+        make_identity(nc, ident_f[:])
+        nc.gpsimd.memset(warm_in[:], 0.0)
+        nc.gpsimd.memset(vec_rows[96:128, :], 0.0)
+        make_identity(nc, ident_b[:])
+
+        x_raw = {}
+        w_bytes = {}
+
+        def load_x(b):
+            x_raw[b] = keep.tile([P, 2, K], BF16, name="x_raw%d" % b)
+            nc.sync.dma_start(out=x_raw[b][:], in_=x_view[b])
+
+        def load_w(q):
+            w_bytes[q] = keep.tile([P, 2, K], U8, name="w_bytes%d" % q)
+            nc.sync.dma_start(out=w_bytes[q][:], in_=w_view[q % 2][q // 2])
+
+        nc.scalar.dma_start(
+            out=scale2[:, 0, :], in_=W_ih0_scale.rearrange("o k -> (o k)").partition_broadcast(P)
+        )
+        load_w(0)
+        load_x(0)
+        load_x(1)
+        load_w(1)
+        nc.sync.dma_start(out=vec_rows[0:32, :], in_=hh_gates.rearrange("(r c) -> r c", c=P))
+        nc.sync.dma_start(out=vec_rows[32:64, :], in_=b_ih0.rearrange("(r c) -> r c", c=P))
+        nc.sync.dma_start(out=vec_rows[64:96, :], in_=b_hh0.rearrange("(r c) -> r c", c=P))
+        nc.sync.dma_start(out=vec_rows[96:104, :], in_=c_init.rearrange("(r c) -> r c", c=P))
+        load_x(2)
+        load_x(3)
+        for q in range(2, NPAIR):
+            load_w(q)
+        nc.scalar.activation(out=warm_out[:], in_=warm_in[:], func=ACT.Sigmoid)
+        nc.scalar.copy(out=scale2[:, 1, :], in_=scale2[:, 0, :])
+
+        def turn_words(bank, rows):
+            words = rows.bitcast(F32)
+            for j in range(2):
+                for u in range(2):
+                    nc.tensor.transpose(
+                        bank[:, u * 256 + j * P : u * 256 + (j + 1) * P],
+                        words[:, j * 256 + u : (j + 1) * 256 : 2],
+                        ident_f[:],
+                    )
+
+        def regroup(grouped, bank, on_vector):
+            dst = grouped.bitcast(F32).rearrange("p (r u) -> p r u", u=2)
+            src = bank.rearrange("p (u r) -> p r u", u=2)
+            if on_vector:
+                nc.vector.tensor_copy(out=dst, in_=src)
+            else:
+                nc.scalar.copy(out=dst, in_=src)
+
+        x_bank = {}
+        x_grouped = {}
+        x_codes = {}
+        x_scales = {}
+
+        def x_transpose(b):
+            x_bank[b] = psum.tile([P, 512], F32, name="x_bank", tag="cT" if b % 2 == 0 else "oT")
+            turn_words(x_bank[b], x_raw[b][:].rearrange("p j k -> p (j k)"))
+
+        def x_copy(b, on_vector):
+            t = b // 2
+            if b % 2 == 0:
+                x_grouped[t] = keep.tile([P, 4 * HALF], BF16, name="x_grouped%d" % t, align_bytes=64)
+            regroup(x_grouped[t][:, (b % 2) * 1024 : (b % 2 + 1) * 1024], x_bank[b][:], on_vector)
+
+        def x_quant(t):
+            x_codes[t] = keep.tile([P, HALF], U32, name="x_codes%d" % t, align_bytes=64)
+            x_scales[t] = keep.tile([P, HALF], U8, name="x_scales%d" % t, align_bytes=64)
+            nc.vector.quantize_mx(
+                out=x_codes[t][:].bitcast(FP8X4), scales=x_scales[t][:], in_=x_grouped[t][:]
+            )
+
+        w_wide = {}
+        w_bank = {}
+        w_grouped = {}
+        w_codes = {}
+        w_scales = {}
+
+        def widen_gate(q, a):
+            if a == 0:
+                w_wide[q] = prep.tile([P, 2 * K], BF16, name="w_wide", tag="w_wide")
+            nc.vector.tensor_tensor(
+                out=w_wide[q][:, a * K : (a + 1) * K],
+                in0=w_bytes[q][:, a, :].bitcast(FP8),
+                in1=scale2[:, 0, :],
+                op=ALU.mult,
+            )
+
+        def widen(q):
+            w_wide[q] = prep.tile([P, 2 * K], BF16, name="w_wide", tag="w_wide")
+            nc.vector.tensor_tensor(
+                out=w_wide[q][:],
+                in0=w_bytes[q][:].rearrange("p a k -> p (a k)").bitcast(FP8),
+                in1=scale2[:].rearrange("p a k -> p (a k)"),
+                op=ALU.mult,
+            )
+
+        def w_transpose(q):
+            w_bank[q] = psum.tile([P, 512], F32, name="w_bank", tag="pa")
+            turn_words(w_bank[q], w_wide[q][:])
+
+        def w_copy(q):
+            w_grouped[q] = prep.tile([P, 1024], BF16, name="w_grouped", tag="w_grouped", align_bytes=64)
+            regroup(w_grouped[q][:], w_bank[q][:], q in VECTOR_COPIES)
+
+        def w_quant(q):
+            w_codes[q] = keep.tile([P, 256], U32, name="w_codes%d" % q, align_bytes=64)
+            w_scales[q] = keep.tile([P, 256], U8, name="w_scales%d" % q, align_bytes=64)
+            nc.vector.quantize_mx(
+                out=w_codes[q][:].bitcast(FP8X4), scales=w_scales[q][:], in_=w_grouped[q][:]
+            )
+
+        vT = psum.tile([P, P], BF16, name="vT", tag="g3")
+
+        def vec_turn():
+            nc.tensor.transpose(vT[:], vec_rows[:], ident_b[:])
+
+        def vec_copy():
+            nc.scalar.copy(out=vec_cols[:], in_=vT[:])
+
+        def vec_add():
+            nc.vector.tensor_tensor(out=bias_tmp[:], in0=vec_cols[:, 32:64], in1=vec_cols[:, 64:96], op=ALU.add)
+            nc.vector.tensor_tensor(out=bias[:], in0=vec_cols[:, 0:32], in1=bias_tmp[:], op=ALU.add)
+
+        gate_bank = {}
+        gate_sb = {}
+
+        def gate_tile(k):
+            q, n = k // 4, k % 4
+            if q % 2 == 0:
+                return q, n % 2, n // 2
+            return q, n // 2, n % 2
+
+        def mm(k):
+            q, a, t = gate_tile(k)
+            gate_bank[k] = psum.tile([P, HALF], F32, name="gate_bank", tag="g%d" % (k % GATE_BANKS))
+            nc.tensor.matmul_mx(
+                out=gate_bank[k][:],
+                lhsT=w_codes[q][:, a * P : (a + 1) * P].bitcast(FP8X4),
+                lhsT_scale=w_scales[q][:, a * P : (a + 1) * P],
+                rhs=x_codes[t][:].bitcast(FP8X4),
+                rhs_scale=x_scales[t][:],
+                start=True,
+                stop=True,
+            )
+
+        def act(k):
+            q, a, t = gate_tile(k)
+            gate, h = 2 * a + q % 2, q // 2
+            if t == 0:
+                gate_sb[(h, gate)] = ep.tile([P, 2 * HALF], F32, name="gate_sb", tag="gate%d" % gate)
+            nc.scalar.activation(
+                out=gate_sb[(h, gate)][:, t * HALF : (t + 1) * HALF],
+                in_=gate_bank[k][:],
+                func=ACT.Tanh if gate == GATE_G else ACT.Sigmoid,
+                bias=bias[:, gate * NH + h : gate * NH + h + 1],
+                scale=1.0,
+            )
+
+        ig_sb = {}
+        fc_sb = {}
+        cT = {}
+        oT = {}
+        tanh_sb = {}
+
+        def ig(h, lo, hi):
+            if lo == 0:
+                ig_sb[h] = ep.tile([P, 2 * HALF], F32, name="ig", tag="ig")
+            nc.vector.tensor_tensor(
+                out=ig_sb[h][:, lo:hi],
+                in0=gate_sb[(h, GATE_I)][:, lo:hi],
+                in1=gate_sb[(h, GATE_G)][:, lo:hi],
+                op=ALU.mult,
+            )
+
+        def fc(h, lo, hi):
+            if lo == 0:
+                fc_sb[h] = ep.tile([P, 2 * HALF], F32, name="fc", tag="fc")
+            nc.vector.tensor_scalar(
+                out=fc_sb[h][:, lo:hi],
+                in0=gate_sb[(h, GATE_F)][:, lo:hi],
+                scalar1=vec_cols[:, 96 + h : 97 + h],
+                scalar2=None,
+                op0=ALU.mult,
+            )
+
+        def turn_c(h, t, tag):
+            cT[(h, t)] = psum.tile([P, HALF], F32, name="cT", tag=tag)
+            for j in range(4):
+                cols = slice(t * HALF + j * P, t * HALF + (j + 1) * P)
+                nc.tensor.matmul(
+                    out=cT[(h, t)][:, j * P : (j + 1) * P], lhsT=ig_sb[h][:, cols], rhs=ident_f[:],
+                    start=True, stop=False, is_transpose=True,
+                )
+                nc.tensor.matmul(
+                    out=cT[(h, t)][:, j * P : (j + 1) * P], lhsT=fc_sb[h][:, cols], rhs=ident_f[:],
+                    start=False, stop=True, is_transpose=True,
+                )
+
+        def turn_o(h, t, tag):
+            oT[(h, t)] = psum.tile([P, HALF], F32, name="oT", tag=tag)
+            for j in range(4):
+                nc.tensor.transpose(
+                    oT[(h, t)][:, j * P : (j + 1) * P],
+                    gate_sb[(h, GATE_O)][:, t * HALF + j * P : t * HALF + (j + 1) * P],
+                    ident_f[:],
+                )
+
+        def tanh_c(h, t, lo, hi):
+            if lo == 0:
+                tanh_sb[(h, t)] = ep.tile([P, HALF], F32, name="tanh_c", tag="tanh_c")
+            nc.scalar.activation(out=tanh_sb[(h, t)][:, lo:hi], in_=cT[(h, t)][:, lo:hi], func=ACT.Tanh)
+
+        def final(h, t, lo, hi):
+            res = ep.tile([P, (hi - lo) // P, P], F32, name="res", tag="res")
+            nc.vector.tensor_tensor(
+                out=res[:].rearrange("p j c -> p (j c)"),
+                in0=oT[(h, t)][:, lo:hi],
+                in1=tanh_sb[(h, t)][:, lo:hi],
+                op=ALU.mult,
+            )
+            nc.sync.dma_start(out=out_view[t][:, lo // P : hi // P, h * P : (h + 1) * P], in_=res[:])
+
+        widen_gate(0, 0)
+        widen_gate(0, 1)
+        x_transpose(0)
+        x_copy(0, False)
+        x_transpose(1)
+        w_transpose(0)
+        vec_turn()
+        widen_gate(1, 0)
+        x_copy(1, False)
+        x_transpose(2)
+        w_copy(0)
+        vec_copy()
+        widen_gate(1, 1)
+        x_quant(0)
+        x_copy(2, False)
+        x_transpose(3)
+        w_quant(0)
+        vec_add()
+        mm(0)
+        mm(1)
+        act(0)
+        x_copy(3, True)
+        act(1)
+        w_transpose(1)
+        x_quant(1)
+        mm(2)
+        mm(3)
+        w_copy(1)
+        widen(2)
+        act(2)
+        w_quant(1)
+        w_transpose(2)
+        mm(4)
+        act(3)
+        mm(6)
+        w_copy(2)
+        mm(5)
+        widen(3)
+        ig(0, 0, 2 * HALF)
+        mm(7)
+        w_quant(2)
+
+        for s in range(1, NPAIR - 1):
+            h = s // 2
+            k = 4 * s
+            if s % 2 == 0:
+                if s + 2 < NPAIR:
+                    w_transpose(s + 2)
+                if s + 3 < NPAIR:
+                    widen(s + 3)
+                act(k)
+                act(k + 2)
+                act(k + 1)
+                if h == NH - 1:
+                    ig(h, 0, HALF)
+                tanh_c(h - 1, 0, 0, HALF)
+                turn_o(h - 1, 0, "oT")
+                mm(k + 4)
+                mm(k + 6)
+                if s + 2 < NPAIR:
+                    w_copy(s + 2)
+                mm(k + 5)
+                act(k + 3)
+                final(h - 1, 0, 0, HALF)
+                mm(k + 7)
+                if s + 2 < NPAIR:
+                    w_quant(s + 2)
+                ig(h, HALF if h == NH - 1 else 0, 2 * HALF)
+                turn_c(h - 1, 1, "cT")
+            else:
+                act(k)
+                if s + 2 < NPAIR:
+                    w_transpose(s + 2)
+                act(k + 1)
+                fc(h, 0, 2 * HALF)
+                act(k + 2)
+                if h > 0:
+                    tanh_c(h - 1, 1, 0, HALF)
+                    turn_o(h - 1, 1, "oT")
+                if s + 2 < NPAIR:
+                    w_copy(s + 2)
+                mm(k + 4)
+                mm(k + 7)
+                mm(k + 6)
+                mm(k + 5)
+                act(k + 3)
+                if s + 3 < NPAIR:
+                    widen(s + 3)
+                if h > 0:
+                    final(h - 1, 1, 0, HALF)
+                turn_c(h, 0, "cT")
+                if s + 2 < NPAIR:
+                    w_quant(s + 2)
+
+        h = NH - 1
+        k = 4 * (NPAIR - 1)
+        turn_o(h - 1, 1, "oT")
+        act(k)
+        fc(h, 0, HALF)
+        act(k + 1)
+        fc(h, HALF, 2 * HALF)
+        act(k + 2)
+        tanh_c(h - 1, 1, 0, HALF)
+        final(h - 1, 1, 0, HALF)
+        turn_c(h, 0, "pa")
+        turn_c(h, 1, "g4")
+        turn_o(h, 0, "g0")
+        act(k + 3)
+        tanh_c(h, 0, 0, HALF)
+        final(h, 0, 0, HALF)
+        turn_o(h, 1, "g1")
+        for lo in range(0, HALF, HALF // 2):
+            tanh_c(h, 1, lo, lo + HALF // 2)
+            final(h, 1, lo, lo + HALF // 2)

@@ -51,6 +51,7 @@ def tile_rdecommunicationlstm_pa_kernel(
         ident_f = const.tile([P, P], F32, name="ident_f")
         ident_b = const.tile([P, P], BF16, name="ident_b")
         scale2 = const.tile([P, 2, K], F32, name="scale2")
+        scale_cols = const.tile([P, 4], F32, name="scale_cols")
 
         make_identity(nc, ident_f[:])
         nc.gpsimd.memset(warm_in[:], 0.0)
@@ -68,9 +69,7 @@ def tile_rdecommunicationlstm_pa_kernel(
             w_bytes[q] = keep.tile([P, 2, K], U8, name="w_bytes%d" % q)
             nc.sync.dma_start(out=w_bytes[q][:], in_=w_view[q % 2][q // 2])
 
-        nc.scalar.dma_start(
-            out=scale2[:, 0, :], in_=W_ih0_scale.rearrange("o k -> (o k)").partition_broadcast(P)
-        )
+        nc.sync.dma_start(out=scale_cols[:], in_=W_ih0_scale.rearrange("o (p c) -> p (o c)", c=4))
         load_w(0)
         load_x(0)
         load_x(1)
@@ -84,6 +83,15 @@ def tile_rdecommunicationlstm_pa_kernel(
         for q in range(2, NPAIR):
             load_w(q)
         nc.scalar.activation(out=warm_out[:], in_=warm_in[:], func=ACT.Sigmoid)
+        scale_bank = psum.tile([P, K], F32, name="scale_bank", tag="g0")
+        for c in range(4):
+            nc.tensor.matmul(
+                out=scale_bank[:, c * P : (c + 1) * P], lhsT=scale_cols[:, c : c + 1].to_broadcast([P, P]), rhs=ident_f[:],
+                start=True, stop=True, is_transpose=True,
+            )
+        nc.scalar.copy(
+            out=scale2[:, 0, :].rearrange("m (n c) -> m n c", c=4), in_=scale_bank[:].rearrange("m (c n) -> m n c", c=4)
+        )
         nc.scalar.copy(out=scale2[:, 1, :], in_=scale2[:, 0, :])
 
         def turn_words(bank, rows):

@@ -22,7 +22,7 @@ GATE_I, GATE_F, GATE_G, GATE_O = 0, 1, 2, 3
 
 NPAIR = 2 * NH
 GATE_BANKS = 5
-VECTOR_COPIES = (4, 6, 8, 10, 12, 14, 15)
+VECTOR_COPIES = (4, 6, 8, 10, 12, 13, 14, 15)
 
 
 def tile_rdecommunicationlstm_pa_kernel(
@@ -30,9 +30,9 @@ def tile_rdecommunicationlstm_pa_kernel(
 ):
     nc = tc.nc
 
-    x_view = regime_vector.rearrange("(b j p) k -> b p j k", b=4, j=2, p=P)
+    x_view = regime_vector.rearrange("(t p i j) k -> t i p j k", t=2, i=2, j=2)
     w_view = W_ih0_bytes.rearrange("(a q h p) k -> q h p a k", a=2, q=2, h=NH, p=P)
-    out_view = out.rearrange("(t j p) c -> t p j c", t=2, j=4, p=P)
+    out_view = out.rearrange("(t p j) c -> t p j c", t=2, j=4)
 
     with ExitStack() as ctx:
         const = ctx.enter_context(tc.tile_pool(name="const", bufs=1))
@@ -63,7 +63,7 @@ def tile_rdecommunicationlstm_pa_kernel(
 
         def load_x(b):
             x_raw[b] = keep.tile([P, 2, K], BF16, name="x_raw%d" % b)
-            nc.sync.dma_start(out=x_raw[b][:], in_=x_view[b])
+            nc.sync.dma_start(out=x_raw[b][:], in_=x_view[b // 2][b % 2])
 
         def load_w(q):
             w_bytes[q] = keep.tile([P, 2, K], U8, name="w_bytes%d" % q)

from contextlib import ExitStack

import concourse.mybir as mybir
from concourse.masks import make_identity

B, K, HID, NG = 1024, 512, 1024, 4
FLOPS = 2 * B * K * NG * HID

F32 = mybir.dt.float32
BF16 = mybir.dt.bfloat16
U32 = mybir.dt.uint32
U8 = mybir.dt.uint8
FP8 = mybir.dt.float8_e4m3fn
FP8X4 = mybir.dt.float8_e4m3fn_x4
ACT = mybir.ActivationFunctionType
ALU = mybir.AluOpType

P = 128
NH = HID // P
HALF = 512
GATE_I, GATE_F, GATE_G, GATE_O = 0, 1, 2, 3

NPAIR = 2 * NH
GATE_BANKS = 5
VECTOR_COPIES = (4, 6, 8, 10, 12, 13, 14, 15)


def tile_rdecommunicationlstm_pa_kernel(
    tc, regime_vector, W_ih0_bytes, W_ih0_scale, hh_gates, b_ih0, b_hh0, c_init, out
):
    nc = tc.nc

    x_view = regime_vector.rearrange("(t p i j) k -> t i p j k", t=2, i=2, j=2)
    w_view = W_ih0_bytes.rearrange("(a q h p) k -> q h p a k", a=2, q=2, h=NH, p=P)
    out_view = out.rearrange("(t p j) c -> t p j c", t=2, j=4)

    with ExitStack() as ctx:
        const = ctx.enter_context(tc.tile_pool(name="const", bufs=1))
        keep = ctx.enter_context(tc.tile_pool(name="keep", bufs=1))
        prep = ctx.enter_context(tc.tile_pool(name="prep", bufs=3))
        ep = ctx.enter_context(tc.tile_pool(name="ep", bufs=4))
        psum = ctx.enter_context(tc.psum_pool(name="psum", bufs=1))
        ctx.enter_context(tc.manual_schedule())

        warm_in = const.tile([P, 1], F32, name="warm_in")
        warm_out = const.tile([P, 1], F32, name="warm_out")
        vec_rows = const.tile([P, P], BF16, name="vec_rows")
        vec_cols = const.tile([P, P], F32, name="vec_cols")
        bias_tmp = const.tile([P, NG * NH], F32, name="bias_tmp")
        bias = const.tile([P, NG * NH], F32, name="bias")
        ident_f = const.tile([P, P], F32, name="ident_f")
        ident_b = const.tile([P, P], BF16, name="ident_b")
        scale2 = const.tile([P, 2, K], F32, name="scale2")
        scale_cols = const.tile([P, 4], F32, name="scale_cols")

        make_identity(nc, ident_f[:])
        nc.gpsimd.memset(warm_in[:], 0.0)
        nc.gpsimd.memset(vec_rows[96:128, :], 0.0)
        make_identity(nc, ident_b[:])

        x_raw = {}
        w_bytes = {}

        def load_x(b):
            x_raw[b] = keep.tile([P, 2, K], BF16, name="x_raw%d" % b)
            nc.sync.dma_start(out=x_raw[b][:], in_=x_view[b // 2][b % 2])

        def load_w(q):
            w_bytes[q] = keep.tile([P, 2, K], U8, name="w_bytes%d" % q)
            nc.sync.dma_start(out=w_bytes[q][:], in_=w_view[q % 2][q // 2])

        nc.sync.dma_start(out=scale_cols[:], in_=W_ih0_scale.rearrange("o (p c) -> p (o c)", c=4))
        load_w(0)
        load_x(0)
        load_x(1)
        load_w(1)
        nc.sync.dma_start(out=vec_rows[0:32, :], in_=hh_gates.rearrange("(r c) -> r c", c=P))
        nc.sync.dma_start(out=vec_rows[32:64, :], in_=b_ih0.rearrange("(r c) -> r c", c=P))
        nc.sync.dma_start(out=vec_rows[64:96, :], in_=b_hh0.rearrange("(r c) -> r c", c=P))
        nc.sync.dma_start(out=vec_rows[96:104, :], in_=c_init.rearrange("(r c) -> r c", c=P))
        load_x(2)
        load_x(3)
        for q in range(2, NPAIR):
            load_w(q)
        nc.scalar.activation(out=warm_out[:], in_=warm_in[:], func=ACT.Sigmoid)
        scale_bank = psum.tile([P, K], F32, name="scale_bank", tag="g0")
        for c in range(4):
            nc.tensor.matmul(
                out=scale_bank[:, c * P : (c + 1) * P], lhsT=scale_cols[:, c : c + 1].to_broadcast([P, P]), rhs=ident_f[:],
                start=True, stop=True, is_transpose=True,
            )
        nc.scalar.copy(
            out=scale2[:, 0, :].rearrange("m (n c) -> m n c", c=4), in_=scale_bank[:].rearrange("m (c n) -> m n c", c=4)
        )
        nc.scalar.copy(out=scale2[:, 1, :], in_=scale2[:, 0, :])

        def turn_words(bank, rows):
            words = rows.bitcast(F32)
            for j in range(2):
                for u in range(2):
                    nc.tensor.transpose(
                        bank[:, u * 256 + j * P : u * 256 + (j + 1) * P],
                        words[:, j * 256 + u : (j + 1) * 256 : 2],
                        ident_f[:],
                    )

        def regroup(grouped, bank, on_vector):
            dst = grouped.bitcast(F32).rearrange("p (r u) -> p r u", u=2)
            src = bank.rearrange("p (u r) -> p r u", u=2)
            if on_vector:
                nc.vector.tensor_copy(out=dst, in_=src)
            else:
                nc.scalar.copy(out=dst, in_=src)

        x_bank = {}
        x_grouped = {}
        x_codes = {}
        x_scales = {}

        def x_transpose(b):
            x_bank[b] = psum.tile([P, 512], F32, name="x_bank", tag="cT" if b % 2 == 0 else "oT")
            turn_words(x_bank[b], x_raw[b][:].rearrange("p j k -> p (j k)"))

        def x_copy(b, on_vector):
            t = b // 2
            if b % 2 == 0:
                x_grouped[t] = keep.tile([P, 4 * HALF], BF16, name="x_grouped%d" % t, align_bytes=64)
            regroup(x_grouped[t][:, (b % 2) * 1024 : (b % 2 + 1) * 1024], x_bank[b][:], on_vector)

        def x_quant(t):
            x_codes[t] = keep.tile([P, HALF], U32, name="x_codes%d" % t, align_bytes=64)
            x_scales[t] = keep.tile([P, HALF], U8, name="x_scales%d" % t, align_bytes=64)
            nc.vector.quantize_mx(
                out=x_codes[t][:].bitcast(FP8X4), scales=x_scales[t][:], in_=x_grouped[t][:]
            )

        w_wide = {}
        w_bank = {}
        w_grouped = {}
        w_codes = {}
        w_scales = {}

        def widen_gate(q, a):
            if a == 0:
                w_wide[q] = prep.tile([P, 2 * K], BF16, name="w_wide", tag="w_wide")
            nc.vector.tensor_tensor(
                out=w_wide[q][:, a * K : (a + 1) * K],
                in0=w_bytes[q][:, a, :].bitcast(FP8),
                in1=scale2[:, 0, :],
                op=ALU.mult,
            )

        def widen(q):
            w_wide[q] = prep.tile([P, 2 * K], BF16, name="w_wide", tag="w_wide")
            nc.vector.tensor_tensor(
                out=w_wide[q][:],
                in0=w_bytes[q][:].rearrange("p a k -> p (a k)").bitcast(FP8),
                in1=scale2[:].rearrange("p a k -> p (a k)"),
                op=ALU.mult,
            )

        def w_transpose(q):
            w_bank[q] = psum.tile([P, 512], F32, name="w_bank", tag="pa")
            turn_words(w_bank[q], w_wide[q][:])

        def w_copy(q):
            w_grouped[q] = prep.tile([P, 1024], BF16, name="w_grouped", tag="w_grouped", align_bytes=64)
            regroup(w_grouped[q][:], w_bank[q][:], q in VECTOR_COPIES)

        def w_quant(q):
            w_codes[q] = keep.tile([P, 256], U32, name="w_codes%d" % q, align_bytes=64)
            w_scales[q] = keep.tile([P, 256], U8, name="w_scales%d" % q, align_bytes=64)
            nc.vector.quantize_mx(
                out=w_codes[q][:].bitcast(FP8X4), scales=w_scales[q][:], in_=w_grouped[q][:]
            )

        vT = psum.tile([P, P], BF16, name="vT", tag="g3")

        def vec_turn():
            nc.tensor.transpose(vT[:], vec_rows[:], ident_b[:])

        def vec_copy():
            nc.scalar.copy(out=vec_cols[:], in_=vT[:])

        def vec_add():
            nc.vector.tensor_tensor(out=bias_tmp[:], in0=vec_cols[:, 32:64], in1=vec_cols[:, 64:96], op=ALU.add)
            nc.vector.tensor_tensor(out=bias[:], in0=vec_cols[:, 0:32], in1=bias_tmp[:], op=ALU.add)

        gate_bank = {}
        gate_sb = {}

        def gate_tile(k):
            q, n = k // 4, k % 4
            if q % 2 == 0:
                return q, n % 2, n // 2
            return q, n // 2, n % 2

        def mm(k):
            q, a, t = gate_tile(k)
            gate_bank[k] = psum.tile([P, HALF], F32, name="gate_bank", tag="g%d" % (k % GATE_BANKS))
            nc.tensor.matmul_mx(
                out=gate_bank[k][:],
                lhsT=w_codes[q][:, a * P : (a + 1) * P].bitcast(FP8X4),
                lhsT_scale=w_scales[q][:, a * P : (a + 1) * P],
                rhs=x_codes[t][:].bitcast(FP8X4),
                rhs_scale=x_scales[t][:],
                start=True,
                stop=True,
            )

        def act(k):
            q, a, t = gate_tile(k)
            gate, h = 2 * a + q % 2, q // 2
            if t == 0:
                gate_sb[(h, gate)] = ep.tile([P, 2 * HALF], F32, name="gate_sb", tag="gate%d" % gate)
            nc.scalar.activation(
                out=gate_sb[(h, gate)][:, t * HALF : (t + 1) * HALF],
                in_=gate_bank[k][:],
                func=ACT.Tanh if gate == GATE_G else ACT.Sigmoid,
                bias=bias[:, gate * NH + h : gate * NH + h + 1],
                scale=1.0,
            )

        ig_sb = {}
        fc_sb = {}
        cT = {}
        oT = {}
        tanh_sb = {}

        def ig(h, lo, hi):
            if lo == 0:
                ig_sb[h] = ep.tile([P, 2 * HALF], F32, name="ig", tag="ig")
            nc.vector.tensor_tensor(
                out=ig_sb[h][:, lo:hi],
                in0=gate_sb[(h, GATE_I)][:, lo:hi],
                in1=gate_sb[(h, GATE_G)][:, lo:hi],
                op=ALU.mult,
            )

        def fc(h, lo, hi):
            if lo == 0:
                fc_sb[h] = ep.tile([P, 2 * HALF], F32, name="fc", tag="fc")
            nc.vector.tensor_scalar(
                out=fc_sb[h][:, lo:hi],
                in0=gate_sb[(h, GATE_F)][:, lo:hi],
                scalar1=vec_cols[:, 96 + h : 97 + h],
                scalar2=None,
                op0=ALU.mult,
            )

        def turn_c(h, t, tag):
            cT[(h, t)] = psum.tile([P, HALF], F32, name="cT", tag=tag)
            for j in range(4):
                cols = slice(t * HALF + j * P, t * HALF + (j + 1) * P)
                nc.tensor.matmul(
                    out=cT[(h, t)][:, j * P : (j + 1) * P], lhsT=ig_sb[h][:, cols], rhs=ident_f[:],
                    start=True, stop=False, is_transpose=True,
                )
                nc.tensor.matmul(
                    out=cT[(h, t)][:, j * P : (j + 1) * P], lhsT=fc_sb[h][:, cols], rhs=ident_f[:],
                    start=False, stop=True, is_transpose=True,
                )

        def turn_o(h, t, tag):
            oT[(h, t)] = psum.tile([P, HALF], F32, name="oT", tag=tag)
            for j in range(4):
                nc.tensor.transpose(
                    oT[(h, t)][:, j * P : (j + 1) * P],
                    gate_sb[(h, GATE_O)][:, t * HALF + j * P : t * HALF + (j + 1) * P],
                    ident_f[:],
                )

        def tanh_c(h, t, lo, hi):
            if lo == 0:
                tanh_sb[(h, t)] = ep.tile([P, HALF], F32, name="tanh_c", tag="tanh_c")
            nc.scalar.activation(out=tanh_sb[(h, t)][:, lo:hi], in_=cT[(h, t)][:, lo:hi], func=ACT.Tanh)

        def final(h, t, lo, hi):
            res = ep.tile([P, (hi - lo) // P, P], F32, name="res", tag="res")
            nc.vector.tensor_tensor(
                out=res[:].rearrange("p j c -> p (j c)"),
                in0=oT[(h, t)][:, lo:hi],
                in1=tanh_sb[(h, t)][:, lo:hi],
                op=ALU.mult,
            )
            nc.sync.dma_start(out=out_view[t][:, lo // P : hi // P, h * P : (h + 1) * P], in_=res[:])

        widen_gate(0, 0)
        widen_gate(0, 1)
        x_transpose(0)
        x_copy(0, False)
        x_transpose(1)
        w_transpose(0)
        vec_turn()
        widen_gate(1, 0)
        x_copy(1, False)
        x_transpose(2)
        w_copy(0)
        vec_copy()
        widen_gate(1, 1)
        x_quant(0)
        x_copy(2, False)
        x_transpose(3)
        w_quant(0)
        vec_add()
        mm(0)
        mm(1)
        act(0)
        x_copy(3, True)
        act(1)
        w_transpose(1)
        x_quant(1)
        mm(2)
        mm(3)
        w_copy(1)
        widen(2)
        act(2)
        w_quant(1)
        w_transpose(2)
        mm(4)
        act(3)
        mm(6)
        w_copy(2)
        mm(5)
        widen(3)
        ig(0, 0, 2 * HALF)
        mm(7)
        w_quant(2)

        for s in range(1, NPAIR - 1):
            h = s // 2
            k = 4 * s
            if s % 2 == 0:
                if s + 2 < NPAIR:
                    w_transpose(s + 2)
                if s + 3 < NPAIR:
                    widen(s + 3)
                act(k)
                act(k + 2)
                act(k + 1)
                if h == NH - 1:
                    ig(h, 0, HALF)
                tanh_c(h - 1, 0, 0, HALF)
                turn_o(h - 1, 0, "oT")
                mm(k + 4)
                mm(k + 6)
                if s + 2 < NPAIR:
                    w_copy(s + 2)
                mm(k + 5)
                act(k + 3)
                final(h - 1, 0, 0, HALF)
                mm(k + 7)
                if s + 2 < NPAIR:
                    w_quant(s + 2)
                ig(h, HALF if h == NH - 1 else 0, 2 * HALF)
                turn_c(h - 1, 1, "cT")
            else:
                act(k)
                if s + 2 < NPAIR:
                    w_transpose(s + 2)
                act(k + 1)
                fc(h, 0, 2 * HALF)
                act(k + 2)
                if h > 0:
                    tanh_c(h - 1, 1, 0, HALF)
                    turn_o(h - 1, 1, "oT")
                if s + 2 < NPAIR:
                    w_copy(s + 2)
                mm(k + 4)
                mm(k + 7)
                mm(k + 6)
                mm(k + 5)
                act(k + 3)
                if s + 3 < NPAIR:
                    widen(s + 3)
                if h > 0:
                    final(h - 1, 1, 0, HALF)
                turn_c(h, 0, "cT")
                if s + 2 < NPAIR:
                    w_quant(s + 2)

        h = NH - 1
        k = 4 * (NPAIR - 1)
        turn_o(h - 1, 1, "oT")
        act(k)
        fc(h, 0, HALF)
        act(k + 1)
        fc(h, HALF, 2 * HALF)
        act(k + 2)
        tanh_c(h - 1, 1, 0, HALF)
        final(h - 1, 1, 0, HALF)
        turn_c(h, 0, "pa")
        turn_c(h, 1, "g4")
        turn_o(h, 0, "g0")
        act(k + 3)
        tanh_c(h, 0, 0, HALF)
        final(h, 0, 0, HALF)
        turn_o(h, 1, "g1")
        for lo in range(0, HALF, HALF // 2):
            tanh_c(h, 1, lo, lo + HALF // 2)
            final(h, 1, lo, lo + HALF // 2)
